import numpy as np
import ml_dtypes


def mxq(x, axis, fmt="e4m3"):
    dtype, down = {"e4m3": (ml_dtypes.float8_e4m3fn, 7), "e5m2": (ml_dtypes.float8_e5m2, 14)}[fmt]
    v = np.moveaxis(np.asarray(x, np.float32).astype(ml_dtypes.bfloat16).astype(np.float64), axis, -1)
    blocks = v.reshape(v.shape[:-1] + (-1, 32))
    amax = np.abs(blocks).max(-1, keepdims=True)
    byte = np.maximum(np.where(amax > 0, np.frexp(amax)[1] - 1 + 127, 0) - down, 1)
    scale = np.exp2(byte - 127.0)
    codes = (blocks / scale).astype(np.float32).astype(dtype).astype(np.float64)
    return np.moveaxis((codes * scale).reshape(v.shape), -1, axis)


WIDE = False


def mx_kscale(k):
    if not WIDE:
        return np.ones(k)
    levels = np.array([20, -20, 10, -10, 0])
    a = np.random.permutation(np.resize(levels, k // 512 * 4)).reshape(k // 512, 4)
    idx = np.arange(k)
    return np.exp2(a[idx // 512, idx % 128 // 32])


BF16 = ml_dtypes.bfloat16


def bf(x):
    return np.asarray(x, np.float32).astype(BF16)


def f64(x):
    return np.asarray(x).astype(np.float64)


B, N, C = 1, 2048, 512
Q = N ** 0.25


def setup_inputs():
    s = mx_kscale(N)[None, :, None]
    msg = bf((1.4 * np.random.standard_normal((B, 1, C)) + 1.2 * np.random.standard_normal((B, N, C))) / Q)
    A0 = bf(np.random.uniform(0.0, 1.0, (B, N, N)) * 2.0 / N ** 0.75)
    h = bf(np.maximum(np.random.standard_normal((B, N, C)) * 1.35, 0.0))
    Ws = bf(np.random.uniform(-1.0, 1.0, (C, C)) * 1.5 / np.sqrt(C))
    b = bf(np.random.uniform(-1.0, 1.0, C) * 0.5)
    g = bf(np.random.standard_normal((B, N, C)) * np.exp2(np.random.randint(-12, 1, (B, N, 1))) * 64.0 / s)
    z = f64(A0) @ f64(msg) + f64(h) @ f64(Ws).T + f64(b)
    return {"A": bf(f64(A0) * s), "msg": msg, "h": h, "Ws": Ws, "b": b,
            "z": np.asarray(z, np.float32), "grad_out": g}


def reference(A, msg, h, Ws, b, z, grad_out):
    dz = f64(grad_out) * (f64(z) > 0.0)
    Aq = mxq(f64(A), 1, "e4m3")
    dq = mxq(dz, 1, "e5m2")
    return np.swapaxes(Aq, 1, 2) @ dq

@@ -1,0 +1,129 @@
+from contextlib import ExitStack
+
+import concourse.mybir as mybir
+
+F32 = mybir.dt.float32
+BF16 = mybir.dt.bfloat16
+U32 = mybir.dt.uint32
+U8 = mybir.dt.uint8
+E4M3_X4 = mybir.dt.float8_e4m3fn_x4
+E5M2_X4 = mybir.dt.float8_e5m2_x4
+ALU = mybir.AluOpType
+
+P = 128
+PACK = 4
+NODES = 2048
+CHANNELS = 512
+PASSES = NODES // (P * PACK)
+BANKS = 8
+ROUNDS = NODES // (BANKS * P)
+ROUND_COLS = BANKS * P
+UNIT = 512
+UNITS_PER_ROUND = ROUND_COLS // UNIT
+WHOLE_PASSES = 2
+
+FLOPS = 2 * NODES * NODES * CHANNELS
+BYTES = NODES * NODES * 2 + NODES * CHANNELS * (4 + 2 + 4)
+
+
+def tile_gcnstacking_pb_v_kernel(tc, A, msg, h, Ws, b, z, grad_out, out):
+    nc = tc.nc
+    a_rows = A.flatten_outer_dims().rearrange("(k p t) j -> k p t j", p=P, t=PACK)
+    z_rows = z.flatten_outer_dims().rearrange("(k p t) c -> k p t c", p=P, t=PACK)
+    g_rows = grad_out.flatten_outer_dims().rearrange("(k p t) c -> k p t c", p=P, t=PACK)
+    out_tiles = out.flatten_outer_dims().rearrange("(m p) c -> m p c", p=P)
+
+    with ExitStack() as ctx:
+        loaded = ctx.enter_context(tc.tile_pool(name="loaded", bufs=1))
+        keep = ctx.enter_context(tc.tile_pool(name="keep", bufs=1))
+        grouped = ctx.enter_context(tc.tile_pool(name="grouped", bufs=4))
+        results = ctx.enter_context(tc.tile_pool(name="results", bufs=ROUNDS * BANKS))
+        psum = ctx.enter_context(tc.psum_pool(name="psum", bufs=BANKS))
+
+        a_raw = [loaded.tile([P, PACK, NODES], BF16, name="a_raw%d" % k) for k in range(PASSES)]
+        z_raw = [loaded.tile([P, PACK, CHANNELS], F32, name="z_raw%d" % k) for k in range(PASSES)]
+        g_raw = [loaded.tile([P, PACK, CHANNELS], BF16, name="g_raw%d" % k) for k in range(PASSES)]
+
+        a_codes = keep.tile([P, PASSES, NODES], U32, align_bytes=64)
+        a_scales = keep.tile([P, PASSES, NODES], U8, align_bytes=64)
+        dz_codes = keep.tile([P, PASSES, CHANNELS], U32, align_bytes=64)
+        dz_scales = keep.tile([P, PASSES, CHANNELS], U8, align_bytes=64)
+
+        left = slice(0, ROUND_COLS)
+        right = slice(ROUND_COLS, NODES)
+        for k in range(PASSES):
+            nc.sync.dma_start(out=g_raw[k][:], in_=g_rows[k])
+            nc.sync.dma_start(out=z_raw[k][:], in_=z_rows[k])
+            if k < WHOLE_PASSES:
+                nc.sync.dma_start(out=a_raw[k][:], in_=a_rows[k])
+            else:
+                nc.sync.dma_start(out=a_raw[k][:, :, left], in_=a_rows[k][:, :, left])
+        for k in range(WHOLE_PASSES, PASSES):
+            nc.sync.dma_start(out=a_raw[k][:, :, right], in_=a_rows[k][:, :, right])
+
+        def quantise_dz(k):
+            dz_grouped = grouped.tile([P, CHANNELS, PACK], BF16, align_bytes=64)
+            nc.vector.scalar_tensor_tensor(
+                out=dz_grouped[:],
+                in0=z_raw[k][:].rearrange("p t c -> p c t"),
+                scalar=0.0,
+                in1=g_raw[k][:].rearrange("p t c -> p c t"),
+                op0=ALU.is_gt,
+                op1=ALU.mult,
+            )
+            nc.vector.quantize_mx(
+                out=dz_codes[:, k, :].bitcast(E5M2_X4),
+                scales=dz_scales[:, k, :],
+                in_=dz_grouped[:].rearrange("p c t -> p (c t)"),
+            )
+
+        def quantise_a(k, r):
+            for u in range(r * UNITS_PER_ROUND, (r + 1) * UNITS_PER_ROUND):
+                cols = slice(u * UNIT, (u + 1) * UNIT)
+                a_grouped = grouped.tile([P, UNIT, PACK], BF16, align_bytes=64)
+                source = a_raw[k][:, :, cols].rearrange("p t (w i) -> p w t i", i=4)
+                target = a_grouped[:].rearrange("p (w i) t -> p w t i", i=4)
+                if u % 2 == 0:
+                    nc.vector.tensor_copy(out=target, in_=source)
+                else:
+                    nc.scalar.copy(out=target, in_=source)
+                nc.vector.quantize_mx(
+                    out=a_codes[:, k, cols].bitcast(E4M3_X4),
+                    scales=a_scales[:, k, cols],
+                    in_=a_grouped[:].rearrange("p w t -> p (w t)"),
+                )
+
+        def multiply(k, r, sums):
+            for m in range(BANKS):
+                cols = slice((r * BANKS + m) * P, (r * BANKS + m + 1) * P)
+                nc.tensor.matmul_mx(
+                    out=sums[m][:],
+                    lhsT=a_codes[:, k, cols].bitcast(E4M3_X4),
+                    lhsT_scale=a_scales[:, k, cols],
+                    rhs=dz_codes[:, k, :].bitcast(E5M2_X4),
+                    rhs_scale=dz_scales[:, k, :],
+                    start=(k == 0),
+                    stop=(k == PASSES - 1),
+                )
+
+        def store(r, sums):
+            for m in range(BANKS):
+                result = results.tile([P, CHANNELS], F32)
+                nc.scalar.copy(out=result[:], in_=sums[m][:])
+                nc.sync.dma_start(out=out_tiles[r * BANKS + m], in_=result[:])
+
+        sums = [psum.tile([P, CHANNELS], F32, name="sums", tag="sums") for m in range(BANKS)]
+        for k in range(PASSES):
+            quantise_dz(k)
+            quantise_a(k, 0)
+            if k < WHOLE_PASSES:
+                quantise_a(k, 1)
+            multiply(k, 0, sums)
+        store(0, sums)
+
+        sums = [psum.tile([P, CHANNELS], F32, name="sums", tag="sums") for m in range(BANKS)]
+        for k in range(PASSES):
+            if k >= WHOLE_PASSES:
+                quantise_a(k, 1)
+            multiply(k, 1, sums)
+        store(1, sums)

@@ -20,7 +20,6 @@ ROUNDS = NODES // (BANKS * P)
 ROUND_COLS = BANKS * P
 UNIT = 512
 UNITS_PER_ROUND = ROUND_COLS // UNIT
-WHOLE_PASSES = 2
 
 FLOPS = 2 * NODES * NODES * CHANNELS
 BYTES = NODES * NODES * 2 + NODES * CHANNELS * (4 + 2 + 4)
@@ -49,17 +48,13 @@ def tile_gcnstacking_pb_v_kernel(tc, A, msg, h, Ws, b, z, grad_out, out):
         dz_codes = keep.tile([P, PASSES, CHANNELS], U32, align_bytes=64)
         dz_scales = keep.tile([P, PASSES, CHANNELS], U8, align_bytes=64)
 
-        left = slice(0, ROUND_COLS)
-        right = slice(ROUND_COLS, NODES)
-        for k in range(PASSES):
-            nc.sync.dma_start(out=g_raw[k][:], in_=g_rows[k])
-            nc.sync.dma_start(out=z_raw[k][:], in_=z_rows[k])
-            if k < WHOLE_PASSES:
-                nc.sync.dma_start(out=a_raw[k][:], in_=a_rows[k])
-            else:
-                nc.sync.dma_start(out=a_raw[k][:, :, left], in_=a_rows[k][:, :, left])
-        for k in range(WHOLE_PASSES, PASSES):
-            nc.sync.dma_start(out=a_raw[k][:, :, right], in_=a_rows[k][:, :, right])
+        for r in range(ROUNDS):
+            cols = slice(r * ROUND_COLS, (r + 1) * ROUND_COLS)
+            for k in range(PASSES):
+                if r == 0:
+                    nc.sync.dma_start(out=g_raw[k][:], in_=g_rows[k])
+                    nc.sync.dma_start(out=z_raw[k][:], in_=z_rows[k])
+                nc.sync.dma_start(out=a_raw[k][:, :, cols], in_=a_rows[k][:, :, cols])
 
         def quantise_dz(k):
             dz_grouped = grouped.tile([P, CHANNELS, PACK], BF16, align_bytes=64)
@@ -109,21 +104,17 @@ def tile_gcnstacking_pb_v_kernel(tc, A, msg, h, Ws, b, z, grad_out, out):
         def store(r, sums):
             for m in range(BANKS):
                 result = results.tile([P, CHANNELS], F32)
-                nc.scalar.copy(out=result[:], in_=sums[m][:])
+                if m % 2 == 0:
+                    nc.scalar.copy(out=result[:], in_=sums[m][:])
+                else:
+                    nc.vector.tensor_copy(out=result[:], in_=sums[m][:])
                 nc.sync.dma_start(out=out_tiles[r * BANKS + m], in_=result[:])
 
-        sums = [psum.tile([P, CHANNELS], F32, name="sums", tag="sums") for m in range(BANKS)]
-        for k in range(PASSES):
-            quantise_dz(k)
-            quantise_a(k, 0)
-            if k < WHOLE_PASSES:
-                quantise_a(k, 1)
-            multiply(k, 0, sums)
-        store(0, sums)
-
-        sums = [psum.tile([P, CHANNELS], F32, name="sums", tag="sums") for m in range(BANKS)]
-        for k in range(PASSES):
-            if k >= WHOLE_PASSES:
-                quantise_a(k, 1)
-            multiply(k, 1, sums)
-        store(1, sums)
+        for r in range(ROUNDS):
+            sums = [psum.tile([P, CHANNELS], F32, name="sums", tag="sums") for m in range(BANKS)]
+            for k in range(PASSES):
+                if r == 0:
+                    quantise_dz(k)
+                quantise_a(k, r)
+                multiply(k, r, sums)
+            store(r, sums)

@@ -39,7 +39,10 @@ def tile_gcnstacking_pb_v_kernel(tc, A, msg, h, Ws, b, z, grad_out, out):
         results = ctx.enter_context(tc.tile_pool(name="results", bufs=ROUNDS * BANKS))
         psum = ctx.enter_context(tc.psum_pool(name="psum", bufs=BANKS))
 
-        a_raw = [loaded.tile([P, PACK, NODES], BF16, name="a_raw%d" % k) for k in range(PASSES)]
+        a_raw = [
+            [loaded.tile([P, PACK, ROUND_COLS], BF16, name="a_raw%d_%d" % (k, r)) for r in range(ROUNDS)]
+            for k in range(PASSES)
+        ]
         z_raw = [loaded.tile([P, PACK, CHANNELS], F32, name="z_raw%d" % k) for k in range(PASSES)]
         g_raw = [loaded.tile([P, PACK, CHANNELS], BF16, name="g_raw%d" % k) for k in range(PASSES)]
 
@@ -54,7 +57,7 @@ def tile_gcnstacking_pb_v_kernel(tc, A, msg, h, Ws, b, z, grad_out, out):
                 if r == 0:
                     nc.sync.dma_start(out=g_raw[k][:], in_=g_rows[k])
                     nc.sync.dma_start(out=z_raw[k][:], in_=z_rows[k])
-                nc.sync.dma_start(out=a_raw[k][:, :, cols], in_=a_rows[k][:, :, cols])
+                nc.sync.dma_start(out=a_raw[k][r][:], in_=a_rows[k][:, :, cols])
 
         def quantise_dz(k):
             dz_grouped = grouped.tile([P, CHANNELS, PACK], BF16, align_bytes=64)
@@ -73,10 +76,10 @@ def tile_gcnstacking_pb_v_kernel(tc, A, msg, h, Ws, b, z, grad_out, out):
             )
 
         def quantise_a(k, r):
-            for u in range(r * UNITS_PER_ROUND, (r + 1) * UNITS_PER_ROUND):
-                cols = slice(u * UNIT, (u + 1) * UNIT)
+            for u in range(UNITS_PER_ROUND):
+                cols = slice(r * ROUND_COLS + u * UNIT, r * ROUND_COLS + (u + 1) * UNIT)
                 a_grouped = grouped.tile([P, UNIT, PACK], BF16, align_bytes=64)
-                source = a_raw[k][:, :, cols].rearrange("p t (w i) -> p w t i", i=4)
+                source = a_raw[k][r][:, :, u * UNIT : (u + 1) * UNIT].rearrange("p t (w i) -> p w t i", i=4)
                 target = a_grouped[:].rearrange("p (w i) t -> p w t i", i=4)
                 if u % 2 == 0:
                     nc.vector.tensor_copy(out=target, in_=source)

@@ -105,12 +105,13 @@ def tile_gcnstacking_pb_v_kernel(tc, A, msg, h, Ws, b, z, grad_out, out):
                 )
 
         def store(r, sums):
+            vector_takes_every = 4 if r == 0 else 2
             for m in range(BANKS):
                 result = results.tile([P, CHANNELS], F32)
-                if m % 2 == 0:
-                    nc.scalar.copy(out=result[:], in_=sums[m][:])
-                else:
+                if m % vector_takes_every == vector_takes_every - 1:
                     nc.vector.tensor_copy(out=result[:], in_=sums[m][:])
+                else:
+                    nc.scalar.copy(out=result[:], in_=sums[m][:])
                 nc.sync.dma_start(out=out_tiles[r * BANKS + m], in_=result[:])
 
         for r in range(ROUNDS):

@@ -81,7 +81,7 @@ def tile_gcnstacking_pb_v_kernel(tc, A, msg, h, Ws, b, z, grad_out, out):
                 a_grouped = grouped.tile([P, UNIT, PACK], BF16, align_bytes=64)
                 source = a_raw[k][r][:, :, u * UNIT : (u + 1) * UNIT].rearrange("p t (w i) -> p w t i", i=4)
                 target = a_grouped[:].rearrange("p (w i) t -> p w t i", i=4)
-                if u % 2 == 0:
+                if u == 0 and (r == 1 or k % 2 == 1):
                     nc.vector.tensor_copy(out=target, in_=source)
                 else:
                     nc.scalar.copy(out=target, in_=source)

@@ -54,10 +54,10 @@ def tile_gcnstacking_pb_v_kernel(tc, A, msg, h, Ws, b, z, grad_out, out):
         for r in range(ROUNDS):
             cols = slice(r * ROUND_COLS, (r + 1) * ROUND_COLS)
             for k in range(PASSES):
+                nc.sync.dma_start(out=a_raw[k][r][:], in_=a_rows[k][:, :, cols])
                 if r == 0:
                     nc.sync.dma_start(out=g_raw[k][:], in_=g_rows[k])
                     nc.sync.dma_start(out=z_raw[k][:], in_=z_rows[k])
-                nc.sync.dma_start(out=a_raw[k][r][:], in_=a_rows[k][:, :, cols])
 
         def quantise_dz(k):
             dz_grouped = grouped.tile([P, CHANNELS, PACK], BF16, align_bytes=64)
@@ -81,7 +81,7 @@ def tile_gcnstacking_pb_v_kernel(tc, A, msg, h, Ws, b, z, grad_out, out):
                 a_grouped = grouped.tile([P, UNIT, PACK], BF16, align_bytes=64)
                 source = a_raw[k][r][:, :, u * UNIT : (u + 1) * UNIT].rearrange("p t (w i) -> p w t i", i=4)
                 target = a_grouped[:].rearrange("p (w i) t -> p w t i", i=4)
-                if u == 0 and (r == 1 or k % 2 == 1):
+                if u == 0 and (r == 1 or k == 0):
                     nc.vector.tensor_copy(out=target, in_=source)
                 else:
                     nc.scalar.copy(out=target, in_=source)

@@ -81,7 +81,7 @@ def tile_gcnstacking_pb_v_kernel(tc, A, msg, h, Ws, b, z, grad_out, out):
                 a_grouped = grouped.tile([P, UNIT, PACK], BF16, align_bytes=64)
                 source = a_raw[k][r][:, :, u * UNIT : (u + 1) * UNIT].rearrange("p t (w i) -> p w t i", i=4)
                 target = a_grouped[:].rearrange("p (w i) t -> p w t i", i=4)
-                if u == 0 and (r == 1 or k == 0):
+                if (r == 0 and k == 0 and u == 0) or (r == 1 and (u == 0 or k == PASSES - 1)):
                     nc.vector.tensor_copy(out=target, in_=source)
                 else:
                     nc.scalar.copy(out=target, in_=source)
@@ -91,34 +91,39 @@ def tile_gcnstacking_pb_v_kernel(tc, A, msg, h, Ws, b, z, grad_out, out):
                     in_=a_grouped[:].rearrange("p w t -> p (w t)"),
                 )
 
-        def multiply(k, r, sums):
-            for m in range(BANKS):
-                cols = slice((r * BANKS + m) * P, (r * BANKS + m + 1) * P)
-                nc.tensor.matmul_mx(
-                    out=sums[m][:],
-                    lhsT=a_codes[:, k, cols].bitcast(E4M3_X4),
-                    lhsT_scale=a_scales[:, k, cols],
-                    rhs=dz_codes[:, k, :].bitcast(E5M2_X4),
-                    rhs_scale=dz_scales[:, k, :],
-                    start=(k == 0),
-                    stop=(k == PASSES - 1),
-                )
+        def multiply(k, r, m, sums):
+            cols = slice((r * BANKS + m) * P, (r * BANKS + m + 1) * P)
+            nc.tensor.matmul_mx(
+                out=sums[m][:],
+                lhsT=a_codes[:, k, cols].bitcast(E4M3_X4),
+                lhsT_scale=a_scales[:, k, cols],
+                rhs=dz_codes[:, k, :].bitcast(E5M2_X4),
+                rhs_scale=dz_scales[:, k, :],
+                start=(k == 0),
+                stop=(k == PASSES - 1),
+            )
 
-        def store(r, sums):
-            vector_takes_every = 4 if r == 0 else 2
-            for m in range(BANKS):
-                result = results.tile([P, CHANNELS], F32)
-                if m % vector_takes_every == vector_takes_every - 1:
-                    nc.vector.tensor_copy(out=result[:], in_=sums[m][:])
-                else:
-                    nc.scalar.copy(out=result[:], in_=sums[m][:])
-                nc.sync.dma_start(out=out_tiles[r * BANKS + m], in_=result[:])
+        def store(r, m, sums):
+            result = results.tile([P, CHANNELS], F32)
+            if r == 1 and m % 2 == 1:
+                nc.vector.tensor_copy(out=result[:], in_=sums[m][:])
+            else:
+                nc.scalar.copy(out=result[:], in_=sums[m][:])
+            nc.sync.dma_start(out=out_tiles[r * BANKS + m], in_=result[:])
 
-        for r in range(ROUNDS):
-            sums = [psum.tile([P, CHANNELS], F32, name="sums", tag="sums") for m in range(BANKS)]
+        sums = [psum.tile([P, CHANNELS], F32, name="sums", tag="sums") for m in range(BANKS)]
+        for k in range(PASSES):
+            quantise_dz(k)
+            quantise_a(k, 0)
+            for m in range(BANKS):
+                multiply(k, 0, m, sums)
+        for m in range(BANKS):
+            store(0, m, sums)
+
+        sums = [psum.tile([P, CHANNELS], F32, name="sums", tag="sums") for m in range(BANKS)]
+        for k in range(PASSES):
+            quantise_a(k, 1)
+        for m in range(BANKS):
             for k in range(PASSES):
-                if r == 0:
-                    quantise_dz(k)
-                quantise_a(k, r)
-                multiply(k, r, sums)
-            store(r, sums)
+                multiply(k, 1, m, sums)
+            store(1, m, sums)

@@ -105,7 +105,7 @@ def tile_gcnstacking_pb_v_kernel(tc, A, msg, h, Ws, b, z, grad_out, out):
 
         def store(r, m, sums):
             result = results.tile([P, CHANNELS], F32)
-            if r == 1 and m % 2 == 1:
+            if r == 1 and m >= BANKS // 2 and m % 2 == 0:
                 nc.vector.tensor_copy(out=result[:], in_=sums[m][:])
             else:
                 nc.scalar.copy(out=result[:], in_=sums[m][:])

@@ -20,6 +20,10 @@ ROUNDS = NODES // (BANKS * P)
 ROUND_COLS = BANKS * P
 UNIT = 512
 UNITS_PER_ROUND = ROUND_COLS // UNIT
+LATE_PASSES = (2, 3)
+
+TENSOR_TAKES = ((0,), (), (2, 1), (3,))
+PAIRED_STORES = (0, 2)
 
 FLOPS = 2 * NODES * NODES * CHANNELS
 BYTES = NODES * NODES * 2 + NODES * CHANNELS * (4 + 2 + 4)
@@ -31,18 +35,29 @@ def tile_gcnstacking_pb_v_kernel(tc, A, msg, h, Ws, b, z, grad_out, out):
     z_rows = z.flatten_outer_dims().rearrange("(k p t) c -> k p t c", p=P, t=PACK)
     g_rows = grad_out.flatten_outer_dims().rearrange("(k p t) c -> k p t c", p=P, t=PACK)
     out_tiles = out.flatten_outer_dims().rearrange("(m p) c -> m p c", p=P)
+    out_pairs = out.flatten_outer_dims().rearrange("(n i p) c -> n p i c", p=P, i=2)
 
     with ExitStack() as ctx:
         loaded = ctx.enter_context(tc.tile_pool(name="loaded", bufs=1))
         keep = ctx.enter_context(tc.tile_pool(name="keep", bufs=1))
         grouped = ctx.enter_context(tc.tile_pool(name="grouped", bufs=4))
-        results = ctx.enter_context(tc.tile_pool(name="results", bufs=ROUNDS * BANKS))
+        results = ctx.enter_context(tc.tile_pool(name="results", bufs=ROUNDS * BANKS - 2 * len(PAIRED_STORES)))
+        pairs = ctx.enter_context(tc.tile_pool(name="pairs", bufs=len(PAIRED_STORES)))
         psum = ctx.enter_context(tc.psum_pool(name="psum", bufs=BANKS))
 
         a_raw = [
-            [loaded.tile([P, PACK, ROUND_COLS], BF16, name="a_raw%d_%d" % (k, r)) for r in range(ROUNDS)]
+            [
+                loaded.tile([P, PACK, ROUND_COLS], BF16, name="a_raw%d_%d" % (k, r))
+                for r in range(ROUNDS)
+                if r == 0 or k not in LATE_PASSES
+            ]
             for k in range(PASSES)
         ]
+        a_late = {
+            (k, u): loaded.tile([P, PACK, UNIT], BF16, name="a_late%d_%d" % (k, u))
+            for k in LATE_PASSES
+            for u in range(UNITS_PER_ROUND)
+        }
         z_raw = [loaded.tile([P, PACK, CHANNELS], F32, name="z_raw%d" % k) for k in range(PASSES)]
         g_raw = [loaded.tile([P, PACK, CHANNELS], BF16, name="g_raw%d" % k) for k in range(PASSES)]
 
@@ -54,10 +69,16 @@ def tile_gcnstacking_pb_v_kernel(tc, A, msg, h, Ws, b, z, grad_out, out):
         for r in range(ROUNDS):
             cols = slice(r * ROUND_COLS, (r + 1) * ROUND_COLS)
             for k in range(PASSES):
+                if r == 1 and k in LATE_PASSES:
+                    continue
                 nc.sync.dma_start(out=a_raw[k][r][:], in_=a_rows[k][:, :, cols])
                 if r == 0:
                     nc.sync.dma_start(out=g_raw[k][:], in_=g_rows[k])
                     nc.sync.dma_start(out=z_raw[k][:], in_=z_rows[k])
+        for u in range(UNITS_PER_ROUND):
+            for k in LATE_PASSES:
+                first = ROUND_COLS + u * UNIT
+                nc.sync.dma_start(out=a_late[(k, u)][:], in_=a_rows[k][:, :, first : first + UNIT])
 
         def quantise_dz(k):
             dz_grouped = grouped.tile([P, CHANNELS, PACK], BF16, align_bytes=64)
@@ -75,11 +96,15 @@ def tile_gcnstacking_pb_v_kernel(tc, A, msg, h, Ws, b, z, grad_out, out):
                 in_=dz_grouped[:].rearrange("p c t -> p (c t)"),
             )
 
-        def quantise_a(k, r):
-            for u in range(UNITS_PER_ROUND):
+        def quantise_a(k, r, units=(0, 1)):
+            for u in units:
                 cols = slice(r * ROUND_COLS + u * UNIT, r * ROUND_COLS + (u + 1) * UNIT)
                 a_grouped = grouped.tile([P, UNIT, PACK], BF16, align_bytes=64)
-                source = a_raw[k][r][:, :, u * UNIT : (u + 1) * UNIT].rearrange("p t (w i) -> p w t i", i=4)
+                if r == 1 and k in LATE_PASSES:
+                    rows = a_late[(k, u)][:]
+                else:
+                    rows = a_raw[k][r][:, :, u * UNIT : (u + 1) * UNIT]
+                source = rows.rearrange("p t (w i) -> p w t i", i=4)
                 target = a_grouped[:].rearrange("p (w i) t -> p w t i", i=4)
                 if (r == 0 and k == 0 and u == 0) or (r == 1 and (u == 0 or k == PASSES - 1)):
                     nc.vector.tensor_copy(out=target, in_=source)
@@ -112,18 +137,29 @@ def tile_gcnstacking_pb_v_kernel(tc, A, msg, h, Ws, b, z, grad_out, out):
             nc.sync.dma_start(out=out_tiles[r * BANKS + m], in_=result[:])
 
         sums = [psum.tile([P, CHANNELS], F32, name="sums", tag="sums") for m in range(BANKS)]
-        for k in range(PASSES):
-            quantise_dz(k)
-            quantise_a(k, 0)
-            for m in range(BANKS):
-                multiply(k, 0, m, sums)
-        for m in range(BANKS):
+        with tc.manual_schedule(engines={mybir.EngineType.PE}):
+            for k in range(PASSES):
+                quantise_dz(k)
+                quantise_a(k, 0)
+                for held in TENSOR_TAKES[k]:
+                    for m in range(BANKS):
+                        multiply(held, 0, m, sums)
+        for first in PAIRED_STORES:
+            pair = pairs.tile([P, 2, CHANNELS], F32)
+            for i in range(2):
+                nc.scalar.copy(out=pair[:, i, :], in_=sums[first + i][:])
+            nc.sync.dma_start(out=out_pairs[first // 2], in_=pair[:])
+        for m in range(2 * len(PAIRED_STORES), BANKS):
             store(0, m, sums)
 
         sums = [psum.tile([P, CHANNELS], F32, name="sums", tag="sums") for m in range(BANKS)]
         for k in range(PASSES):
-            quantise_a(k, 1)
-        for m in range(BANKS):
-            for k in range(PASSES):
-                multiply(k, 1, m, sums)
-            store(1, m, sums)
+            if k not in LATE_PASSES:
+                quantise_a(k, 1)
+        for u in range(UNITS_PER_ROUND):
+            for k in LATE_PASSES:
+                quantise_a(k, 1, (u,))
+            for m in range(u * BANKS // 2, (u + 1) * BANKS // 2):
+                for k in range(PASSES):
+                    multiply(k, 1, m, sums)
+                store(1, m, sums)

@@ -23,7 +23,8 @@ UNITS_PER_ROUND = ROUND_COLS // UNIT
 LATE_PASSES = (2, 3)
 
 TENSOR_TAKES = ((0,), (), (2, 1), (3,))
-PAIRED_STORES = (0, 2)
+SPLIT_LOAD = (0, 1)
+PAIRED_STORES = (0, 2, 4)
 
 FLOPS = 2 * NODES * NODES * CHANNELS
 BYTES = NODES * NODES * 2 + NODES * CHANNELS * (4 + 2 + 4)
@@ -49,10 +50,11 @@ def tile_gcnstacking_pb_v_kernel(tc, A, msg, h, Ws, b, z, grad_out, out):
             [
                 loaded.tile([P, PACK, ROUND_COLS], BF16, name="a_raw%d_%d" % (k, r))
                 for r in range(ROUNDS)
-                if r == 0 or k not in LATE_PASSES
+                if r == 0 or (k not in LATE_PASSES and (k, r) != SPLIT_LOAD)
             ]
             for k in range(PASSES)
         ]
+        a_split = [loaded.tile([P, PACK, UNIT], BF16, name="a_split%d" % u) for u in range(UNITS_PER_ROUND)]
         a_late = {
             (k, u): loaded.tile([P, PACK, UNIT], BF16, name="a_late%d_%d" % (k, u))
             for k in LATE_PASSES
@@ -70,6 +72,11 @@ def tile_gcnstacking_pb_v_kernel(tc, A, msg, h, Ws, b, z, grad_out, out):
             cols = slice(r * ROUND_COLS, (r + 1) * ROUND_COLS)
             for k in range(PASSES):
                 if r == 1 and k in LATE_PASSES:
+                    continue
+                if (k, r) == SPLIT_LOAD:
+                    for u in (1, 0):
+                        first = r * ROUND_COLS + u * UNIT
+                        nc.sync.dma_start(out=a_split[u][:], in_=a_rows[k][:, :, first : first + UNIT])
                     continue
                 nc.sync.dma_start(out=a_raw[k][r][:], in_=a_rows[k][:, :, cols])
                 if r == 0:
@@ -102,6 +109,8 @@ def tile_gcnstacking_pb_v_kernel(tc, A, msg, h, Ws, b, z, grad_out, out):
                 a_grouped = grouped.tile([P, UNIT, PACK], BF16, align_bytes=64)
                 if r == 1 and k in LATE_PASSES:
                     rows = a_late[(k, u)][:]
+                elif (k, r) == SPLIT_LOAD:
+                    rows = a_split[u][:]
                 else:
                     rows = a_raw[k][r][:, :, u * UNIT : (u + 1) * UNIT]
                 source = rows.rearrange("p t (w i) -> p w t i", i=4)

from contextlib import ExitStack

import concourse.mybir as mybir

F32 = mybir.dt.float32
BF16 = mybir.dt.bfloat16
U32 = mybir.dt.uint32
U8 = mybir.dt.uint8
E4M3_X4 = mybir.dt.float8_e4m3fn_x4
E5M2_X4 = mybir.dt.float8_e5m2_x4
ALU = mybir.AluOpType

P = 128
PACK = 4
NODES = 2048
CHANNELS = 512
PASSES = NODES // (P * PACK)
BANKS = 8
ROUNDS = NODES // (BANKS * P)
ROUND_COLS = BANKS * P
UNIT = 512
UNITS_PER_ROUND = ROUND_COLS // UNIT
LATE_PASSES = (2, 3)

TENSOR_TAKES = ((0,), (), (2, 1), (3,))
SPLIT_LOAD = (0, 1)
PAIRED_STORES = (0, 2, 4)

FLOPS = 2 * NODES * NODES * CHANNELS
BYTES = NODES * NODES * 2 + NODES * CHANNELS * (4 + 2 + 4)


def tile_gcnstacking_pb_v_kernel(tc, A, msg, h, Ws, b, z, grad_out, out):
    nc = tc.nc
    a_rows = A.flatten_outer_dims().rearrange("(k p t) j -> k p t j", p=P, t=PACK)
    z_rows = z.flatten_outer_dims().rearrange("(k p t) c -> k p t c", p=P, t=PACK)
    g_rows = grad_out.flatten_outer_dims().rearrange("(k p t) c -> k p t c", p=P, t=PACK)
    out_tiles = out.flatten_outer_dims().rearrange("(m p) c -> m p c", p=P)
    out_pairs = out.flatten_outer_dims().rearrange("(n i p) c -> n p i c", p=P, i=2)

    with ExitStack() as ctx:
        loaded = ctx.enter_context(tc.tile_pool(name="loaded", bufs=1))
        keep = ctx.enter_context(tc.tile_pool(name="keep", bufs=1))
        grouped = ctx.enter_context(tc.tile_pool(name="grouped", bufs=4))
        results = ctx.enter_context(tc.tile_pool(name="results", bufs=ROUNDS * BANKS - 2 * len(PAIRED_STORES)))
        pairs = ctx.enter_context(tc.tile_pool(name="pairs", bufs=len(PAIRED_STORES)))
        psum = ctx.enter_context(tc.psum_pool(name="psum", bufs=BANKS))

        a_raw = [
            [
                loaded.tile([P, PACK, ROUND_COLS], BF16, name="a_raw%d_%d" % (k, r))
                for r in range(ROUNDS)
                if r == 0 or (k not in LATE_PASSES and (k, r) != SPLIT_LOAD)
            ]
            for k in range(PASSES)
        ]
        a_split = [loaded.tile([P, PACK, UNIT], BF16, name="a_split%d" % u) for u in range(UNITS_PER_ROUND)]
        a_late = {
            (k, u): loaded.tile([P, PACK, UNIT], BF16, name="a_late%d_%d" % (k, u))
            for k in LATE_PASSES
            for u in range(UNITS_PER_ROUND)
        }
        z_raw = [loaded.tile([P, PACK, CHANNELS], F32, name="z_raw%d" % k) for k in range(PASSES)]
        g_raw = [loaded.tile([P, PACK, CHANNELS], BF16, name="g_raw%d" % k) for k in range(PASSES)]

        a_codes = keep.tile([P, PASSES, NODES], U32, align_bytes=64)
        a_scales = keep.tile([P, PASSES, NODES], U8, align_bytes=64)
        dz_codes = keep.tile([P, PASSES, CHANNELS], U32, align_bytes=64)
        dz_scales = keep.tile([P, PASSES, CHANNELS], U8, align_bytes=64)

        for r in range(ROUNDS):
            cols = slice(r * ROUND_COLS, (r + 1) * ROUND_COLS)
            for k in range(PASSES):
                if r == 1 and k in LATE_PASSES:
                    continue
                if (k, r) == SPLIT_LOAD:
                    for u in (1, 0):
                        first = r * ROUND_COLS + u * UNIT
                        nc.sync.dma_start(out=a_split[u][:], in_=a_rows[k][:, :, first : first + UNIT])
                    continue
                nc.sync.dma_start(out=a_raw[k][r][:], in_=a_rows[k][:, :, cols])
                if r == 0:
                    nc.sync.dma_start(out=g_raw[k][:], in_=g_rows[k])
                    nc.sync.dma_start(out=z_raw[k][:], in_=z_rows[k])
        for u in range(UNITS_PER_ROUND):
            for k in LATE_PASSES:
                first = ROUND_COLS + u * UNIT
                nc.sync.dma_start(out=a_late[(k, u)][:], in_=a_rows[k][:, :, first : first + UNIT])

        def quantise_dz(k):
            dz_grouped = grouped.tile([P, CHANNELS, PACK], BF16, align_bytes=64)
            nc.vector.scalar_tensor_tensor(
                out=dz_grouped[:],
                in0=z_raw[k][:].rearrange("p t c -> p c t"),
                scalar=0.0,
                in1=g_raw[k][:].rearrange("p t c -> p c t"),
                op0=ALU.is_gt,
                op1=ALU.mult,
            )
            nc.vector.quantize_mx(
                out=dz_codes[:, k, :].bitcast(E5M2_X4),
                scales=dz_scales[:, k, :],
                in_=dz_grouped[:].rearrange("p c t -> p (c t)"),
            )

        def quantise_a(k, r, units=(0, 1)):
            for u in units:
                cols = slice(r * ROUND_COLS + u * UNIT, r * ROUND_COLS + (u + 1) * UNIT)
                a_grouped = grouped.tile([P, UNIT, PACK], BF16, align_bytes=64)
                if r == 1 and k in LATE_PASSES:
                    rows = a_late[(k, u)][:]
                elif (k, r) == SPLIT_LOAD:
                    rows = a_split[u][:]
                else:
                    rows = a_raw[k][r][:, :, u * UNIT : (u + 1) * UNIT]
                source = rows.rearrange("p t (w i) -> p w t i", i=4)
                target = a_grouped[:].rearrange("p (w i) t -> p w t i", i=4)
                if (r == 0 and k == 0 and u == 0) or (r == 1 and (u == 0 or k == PASSES - 1)):
                    nc.vector.tensor_copy(out=target, in_=source)
                else:
                    nc.scalar.copy(out=target, in_=source)
                nc.vector.quantize_mx(
                    out=a_codes[:, k, cols].bitcast(E4M3_X4),
                    scales=a_scales[:, k, cols],
                    in_=a_grouped[:].rearrange("p w t -> p (w t)"),
                )

        def multiply(k, r, m, sums):
            cols = slice((r * BANKS + m) * P, (r * BANKS + m + 1) * P)
            nc.tensor.matmul_mx(
                out=sums[m][:],
                lhsT=a_codes[:, k, cols].bitcast(E4M3_X4),
                lhsT_scale=a_scales[:, k, cols],
                rhs=dz_codes[:, k, :].bitcast(E5M2_X4),
                rhs_scale=dz_scales[:, k, :],
                start=(k == 0),
                stop=(k == PASSES - 1),
            )

        def store(r, m, sums):
            result = results.tile([P, CHANNELS], F32)
            if r == 1 and m >= BANKS // 2 and m % 2 == 0:
                nc.vector.tensor_copy(out=result[:], in_=sums[m][:])
            else:
                nc.scalar.copy(out=result[:], in_=sums[m][:])
            nc.sync.dma_start(out=out_tiles[r * BANKS + m], in_=result[:])

        sums = [psum.tile([P, CHANNELS], F32, name="sums", tag="sums") for m in range(BANKS)]
        with tc.manual_schedule(engines={mybir.EngineType.PE}):
            for k in range(PASSES):
                quantise_dz(k)
                quantise_a(k, 0)
                for held in TENSOR_TAKES[k]:
                    for m in range(BANKS):
                        multiply(held, 0, m, sums)
        for first in PAIRED_STORES:
            pair = pairs.tile([P, 2, CHANNELS], F32)
            for i in range(2):
                nc.scalar.copy(out=pair[:, i, :], in_=sums[first + i][:])
            nc.sync.dma_start(out=out_pairs[first // 2], in_=pair[:])
        for m in range(2 * len(PAIRED_STORES), BANKS):
            store(0, m, sums)

        sums = [psum.tile([P, CHANNELS], F32, name="sums", tag="sums") for m in range(BANKS)]
        for k in range(PASSES):
            if k not in LATE_PASSES:
                quantise_a(k, 1)
        for u in range(UNITS_PER_ROUND):
            for k in LATE_PASSES:
                quantise_a(k, 1, (u,))
            for m in range(u * BANKS // 2, (u + 1) * BANKS // 2):
                for k in range(PASSES):
                    multiply(k, 1, m, sums)
                store(1, m, sums)
